import numpy as np
import ml_dtypes


def mxq(x, axis, fmt="e4m3"):
    dtype, down = {"e4m3": (ml_dtypes.float8_e4m3fn, 7), "e5m2": (ml_dtypes.float8_e5m2, 14)}[fmt]
    v = np.moveaxis(np.asarray(x, np.float32).astype(ml_dtypes.bfloat16).astype(np.float64), axis, -1)
    blocks = v.reshape(v.shape[:-1] + (-1, 32))
    amax = np.abs(blocks).max(-1, keepdims=True)
    byte = np.maximum(np.where(amax > 0, np.frexp(amax)[1] - 1 + 127, 0) - down, 1)
    scale = np.exp2(byte - 127.0)
    codes = (blocks / scale).astype(np.float32).astype(dtype).astype(np.float64)
    return np.moveaxis((codes * scale).reshape(v.shape), -1, axis)


WIDE = False


def mx_kscale(k):
    if not WIDE:
        return np.ones(k)
    levels = np.array([10, -10, 5, -5, 0])
    if k % 512:
        return np.exp2(np.random.permutation(np.resize(levels, k // 32))).repeat(32)
    a = np.empty((k // 512, 16))
    for p in range(k // 512):
        a[p, :8] = np.random.permutation(np.resize(levels, 8))
        for g in range(8):
            far = levels[np.abs(levels - a[p, g]) >= 10]
            a[p, g + 8] = far[np.random.randint(len(far))]
    return np.exp2(a.ravel()).repeat(32)


BF16 = ml_dtypes.bfloat16


def bf(x):
    return np.asarray(x, np.float32).astype(BF16)


def f64(x):
    return np.asarray(x).astype(np.float64)


B, N, F, O, E, K = 16, 512, 256, 64, 16, 3


def normalize_adj(a):
    a = np.maximum(a, 0.0) + np.eye(N)[None, :, :]
    d = np.maximum(a.sum(-1), 1e-6)
    r = d ** -0.5
    return r[:, :, None] * a * r[:, None, :]


def setup_inputs():
    s = mx_kscale(N)
    u = (s / s.min()) ** 2
    x = 0.7 * np.random.standard_normal((B, N, F)) + 0.7 * np.random.standard_normal((B, 1, F))
    x = x * (s / s.max())[None, :, None]
    a0 = 0.5 * (np.random.standard_normal((B, N, N)) - 1.0)
    a = u[None, :, None] * a0
    i = np.arange(N)
    a[:, i, i] = u[None, :] * (np.maximum(a0[:, i, i], 0.0) + 1.0) - 1.0
    return {"A": bf(a), "x": bf(x)}


def reference(A, x):
    a_hat = normalize_adj(f64(A))
    a_left = mxq(a_hat, 2, "e4m3")
    xq = mxq(f64(x), 1, "e4m3")
    t2 = 2.0 * (a_left @ mxq(a_hat, 1, "e4m3")) - np.eye(N)[None, :, :]
    xg1 = a_left @ xq
    xg2 = mxq(t2, 2, "e4m3") @ xq
    return np.stack([xg1, xg2], axis=1)

@@ -1,0 +1,255 @@
+from contextlib import ExitStack
+
+import concourse.mybir as mybir
+from concourse.masks import make_identity
+
+F32 = mybir.dt.float32
+BF16 = mybir.dt.bfloat16
+U32 = mybir.dt.uint32
+U8 = mybir.dt.uint8
+FP8X4 = mybir.dt.float8_e4m3fn_x4
+ALU = mybir.AluOpType
+ACT = mybir.ActivationFunctionType
+
+GRAPHS = 16
+NODES = 512
+FEATS = 256
+P = 128
+PACK = 4
+
+RIGHT_QUARTERS_ON_VECTOR = 2
+LOADS_AHEAD = 4
+
+FLOPS = GRAPHS * 2 * (NODES * NODES * NODES + 2 * NODES * NODES * FEATS)
+
+
+def rows_by_node(dram):
+    return dram.rearrange("(p t) w -> p t w", t=PACK)
+
+
+def in_runs(view):
+    return view.rearrange("p (c i) s -> p c s i", i=4)
+
+
+def quantise(nc, pool, grouped, width, name):
+    codes = pool.tile([P, width], U32, align_bytes=64, name=name + "_codes")
+    scales = pool.tile([P, width], U8, align_bytes=64, name=name + "_scales")
+    nc.vector.quantize_mx(out=codes[:].bitcast(FP8X4), scales=scales[:], in_=grouped)
+    return codes, scales
+
+
+def tile_dygcn_pa_t_kernel(tc, A, x, out):
+    nc = tc.nc
+    with ExitStack() as stack:
+        const = stack.enter_context(tc.tile_pool(name="const", bufs=1))
+        loads = stack.enter_context(tc.tile_pool(name="loads", bufs=LOADS_AHEAD + 2))
+        work = stack.enter_context(tc.tile_pool(name="work", bufs=2))
+        small = stack.enter_context(tc.tile_pool(name="small", bufs=3))
+        mx = stack.enter_context(tc.tile_pool(name="mx", bufs=3))
+        results = stack.enter_context(tc.tile_pool(name="results", bufs=4))
+        ps_row = stack.enter_context(tc.psum_pool(name="ps_row", bufs=1))
+        ps_tr = stack.enter_context(tc.psum_pool(name="ps_tr", bufs=2))
+        ps_t2 = stack.enter_context(tc.psum_pool(name="ps_t2", bufs=3))
+        ps_out = stack.enter_context(tc.psum_pool(name="ps_out", bufs=2))
+
+        ident_f32 = const.tile([P, P], F32)
+        make_identity(nc, ident_f32[:])
+        eye_t2 = const.tile([P, PACK, P, PACK], BF16)
+        nc.vector.memset(eye_t2[:], 0.0)
+        for c in range(PACK):
+            nc.vector.tensor_copy(out=eye_t2[:, c, :, c], in_=ident_f32[:])
+
+        live = {}
+
+        def load(b):
+            a_raw = loads.tile([P, PACK, NODES], BF16)
+            for h in range(2):
+                nc.sync.dma_start(out=a_raw[:, 2 * h : 2 * h + 2, :], in_=rows_by_node(A[b])[:, 2 * h : 2 * h + 2, :])
+            x_raw = loads.tile([P, PACK, FEATS], BF16)
+            nc.sync.dma_start(out=x_raw[:], in_=rows_by_node(x[b]))
+            live["a_raw", b] = a_raw
+            live["x_raw", b] = x_raw
+
+        def positive_part(b):
+            a_raw = live["a_raw", b]
+            pos = work.tile([P, PACK, NODES], F32)
+            rowsum = small.tile([P, PACK], F32)
+            for t in range(PACK):
+                nc.scalar.activation(
+                    out=pos[:, t, :], in_=a_raw[:, t, :], func=ACT.Relu, accum_out=rowsum[:, t : t + 1]
+                )
+            for t in range(PACK):
+                diag = pos[:, t, :].rearrange("p (q e) -> p q e", e=PACK)[:, :, t]
+                nc.gpsimd.tensor_tensor(out=diag, in0=diag, in1=ident_f32[:], op=ALU.add)
+            root_deg = small.tile([P, PACK], F32)
+            nc.scalar.activation(out=root_deg[:], in_=rowsum[:], func=ACT.Sqrt, bias=1.0)
+            live["pos", b] = pos
+            live["root_deg", b] = root_deg
+
+        def inverse_root(b):
+            r = small.tile([P, PACK], F32)
+            nc.vector.reciprocal(out=r[:], in_=live["root_deg", b][:])
+            live["r", b] = r
+
+        def spread_r(b):
+            r = live["r", b]
+            r_row = ps_row.tile([P, NODES], F32)
+            for t in range(PACK):
+                nc.tensor.transpose(
+                    r_row[:].rearrange("p (q e) -> p q e", e=PACK)[:, :, t],
+                    r[:, t : t + 1].to_broadcast([P, P]),
+                    ident_f32[:],
+                )
+            live["r_row", b] = r_row
+
+        def scale(b):
+            a_hat = work.tile([P, PACK, NODES], BF16)
+            for t in range(PACK):
+                nc.vector.scalar_tensor_tensor(
+                    out=a_hat[:, t, :],
+                    in0=live["pos", b][:, t, :],
+                    scalar=live["r", b][:, t : t + 1],
+                    in1=live["r_row", b][:],
+                    op0=ALU.mult,
+                    op1=ALU.mult,
+                )
+            live["a_hat", b] = a_hat
+
+        def regroup_right(b):
+            right_grouped = work.tile([P, NODES * PACK], BF16, align_bytes=64)
+            right_words = right_grouped[:].rearrange("p (t q s) -> p t q s", t=PACK, s=PACK)
+            columns = live["a_hat", b][:].rearrange("p s (q e) -> p e q s", e=PACK)
+            for t in range(PACK):
+                copy = nc.vector.tensor_copy if t < RIGHT_QUARTERS_ON_VECTOR else nc.scalar.copy
+                copy(out=in_runs(right_words[:, t, :, :]), in_=in_runs(columns[:, t, :, :]))
+            live["right_grouped", b] = right_grouped
+
+        def flip(b):
+            for h in range(2):
+                flipped = ps_tr.tile([P, 2, 2, P], F32)
+                for c in range(2):
+                    row_words = live["a_hat", b][:, 2 * h + c, :].bitcast(F32)
+                    for u in range(2):
+                        nc.tensor.transpose(flipped[:, c, u, :], row_words[:, u : 2 * P : 2], ident_f32[:])
+                live["flipped", b, h] = flipped
+
+        def regroup_left(b):
+            left_grouped = work.tile([P, NODES * PACK], BF16, align_bytes=64)
+            left_words = left_grouped[:].bitcast(F32).rearrange("p (h c n u) -> p h c n u", h=2, c=2, u=2)
+            for h in range(2):
+                nc.scalar.copy(
+                    out=left_words[:, h, :, :, :], in_=live["flipped", b, h][:].rearrange("p c u n -> p c n u")
+                )
+            live["left_grouped", b] = left_grouped
+
+        def regroup_x(b):
+            x_grouped = work.tile([P, FEATS * PACK], BF16, align_bytes=64)
+            nc.scalar.copy(
+                out=in_runs(x_grouped[:].rearrange("p (f s) -> p f s", s=PACK)),
+                in_=in_runs(live["x_raw", b][:].rearrange("p s f -> p f s")),
+            )
+            live["x_grouped", b] = x_grouped
+
+        def square(b, c):
+            right_codes, right_scales = live["right", b]
+            left_codes, left_scales = live["left", b]
+            n_cols = slice(c * P, (c + 1) * P)
+            squared = ps_t2.tile([P, PACK, P], F32)
+            for t in range(PACK):
+                j_cols = slice(t * P, (t + 1) * P)
+                nc.tensor.matmul_mx(
+                    out=squared[:, t, :],
+                    lhsT=right_codes[:, j_cols].bitcast(FP8X4),
+                    lhsT_scale=right_scales[:, j_cols],
+                    rhs=left_codes[:, n_cols].bitcast(FP8X4),
+                    rhs_scale=left_scales[:, n_cols],
+                    start=True,
+                    stop=True,
+                )
+            live["squared", b, c] = squared
+
+        def chebyshev(b, c):
+            if c == 0:
+                live["t2_grouped", b] = work.tile([P, NODES * PACK], BF16, align_bytes=64, name="t2_grouped")
+            nc.vector.scalar_tensor_tensor(
+                out=live["t2_grouped", b][:].rearrange("p (c n t) -> p c n t", c=PACK, t=PACK)[:, c, :, :],
+                in0=live["squared", b, c][:].rearrange("p t n -> p n t"),
+                scalar=2.0,
+                in1=eye_t2[:, c, :, :],
+                op0=ALU.mult,
+                op1=ALU.subtract,
+            )
+
+        def times_x(b, name):
+            codes, scales = live[name, b]
+            x_codes, x_scales = live["x", b]
+            for h in range(2):
+                acc = ps_out.tile([P, 2, FEATS], F32)
+                for c in range(2):
+                    n_cols = slice((2 * h + c) * P, (2 * h + c + 1) * P)
+                    nc.tensor.matmul_mx(
+                        out=acc[:, c, :],
+                        lhsT=codes[:, n_cols].bitcast(FP8X4),
+                        lhsT_scale=scales[:, n_cols],
+                        rhs=x_codes[:].bitcast(FP8X4),
+                        rhs_scale=x_scales[:],
+                        start=True,
+                        stop=True,
+                    )
+                live["acc", b, h] = acc
+
+        def store(b, which):
+            result = results.tile([P, PACK, FEATS], F32)
+            for h in range(2):
+                nc.scalar.copy(out=result[:, 2 * h : 2 * h + 2, :], in_=live["acc", b, h][:])
+                nc.sync.dma_start(
+                    out=rows_by_node(out[b, which])[:, 2 * h : 2 * h + 2, :], in_=result[:, 2 * h : 2 * h + 2, :]
+                )
+
+        def quantise_as(b, name, width):
+            live[name, b] = quantise(nc, mx, live[name + "_grouped", b][:], width, name)
+
+        with tc.manual_schedule():
+            for b in range(LOADS_AHEAD):
+                load(b)
+            for i in range(-2, GRAPHS + 1):
+                front, middle, back, last = i + 2, i + 1, i, i - 1
+                if front + LOADS_AHEAD < GRAPHS:
+                    load(front + LOADS_AHEAD)
+                if 0 <= last:
+                    times_x(last, "t2")
+                if 0 <= middle < GRAPHS:
+                    scale(middle)
+                if front < GRAPHS:
+                    positive_part(front)
+                if 0 <= back < GRAPHS:
+                    for c in range(PACK - 1):
+                        square(back, c)
+                if 0 <= last:
+                    store(last, 1)
+                if 0 <= middle < GRAPHS:
+                    flip(middle)
+                if 0 <= back < GRAPHS:
+                    for c in range(PACK - 1):
+                        chebyshev(back, c)
+                    square(back, PACK - 1)
+                    chebyshev(back, PACK - 1)
+                if 0 <= middle < GRAPHS:
+                    regroup_left(middle)
+                if front < GRAPHS:
+                    inverse_root(front)
+                if 0 <= back < GRAPHS:
+                    times_x(back, "left")
+                if front < GRAPHS:
+                    spread_r(front)
+                if 0 <= middle < GRAPHS:
+                    regroup_right(middle)
+                if 0 <= back < GRAPHS:
+                    store(back, 0)
+                    quantise_as(back, "t2", NODES)
+                if 0 <= middle < GRAPHS:
+                    quantise_as(middle, "x", FEATS)
+                    quantise_as(middle, "left", NODES)
+                    quantise_as(middle, "right", NODES)
+                if front < GRAPHS:
+                    regroup_x(front)

@@ -27,6 +27,10 @@ def rows_by_node(dram):
     return dram.rearrange("(p t) w -> p t w", t=PACK)
 
 
+def in_column_order(row):
+    return row.rearrange("p (u q e) -> p u q e", u=2, e=2)
+
+
 def in_runs(view):
     return view.rearrange("p (c i) s -> p c s i", i=4)
 
@@ -47,6 +51,7 @@ def tile_dygcn_pa_t_kernel(tc, A, x, out):
         small = stack.enter_context(tc.tile_pool(name="small", bufs=3))
         mx = stack.enter_context(tc.tile_pool(name="mx", bufs=3))
         results = stack.enter_context(tc.tile_pool(name="results", bufs=4))
+        x_work = stack.enter_context(tc.tile_pool(name="x_work", bufs=1))
         ps_row = stack.enter_context(tc.psum_pool(name="ps_row", bufs=1))
         ps_tr = stack.enter_context(tc.psum_pool(name="ps_tr", bufs=2))
         ps_t2 = stack.enter_context(tc.psum_pool(name="ps_t2", bufs=3))
@@ -76,10 +81,13 @@ def tile_dygcn_pa_t_kernel(tc, A, x, out):
             rowsum = small.tile([P, PACK], F32)
             for t in range(PACK):
                 nc.scalar.activation(
-                    out=pos[:, t, :], in_=a_raw[:, t, :], func=ACT.Relu, accum_out=rowsum[:, t : t + 1]
+                    out=in_column_order(pos[:, t, :]),
+                    in_=a_raw[:, t, :].rearrange("p (q u e) -> p u q e", u=2, e=2),
+                    func=ACT.Relu,
+                    accum_out=rowsum[:, t : t + 1],
                 )
             for t in range(PACK):
-                diag = pos[:, t, :].rearrange("p (q e) -> p q e", e=PACK)[:, :, t]
+                diag = in_column_order(pos[:, t, :])[:, t // 2, :, t % 2]
                 nc.gpsimd.tensor_tensor(out=diag, in0=diag, in1=ident_f32[:], op=ALU.add)
             root_deg = small.tile([P, PACK], F32)
             nc.scalar.activation(out=root_deg[:], in_=rowsum[:], func=ACT.Sqrt, bias=1.0)
@@ -96,7 +104,7 @@ def tile_dygcn_pa_t_kernel(tc, A, x, out):
             r_row = ps_row.tile([P, NODES], F32)
             for t in range(PACK):
                 nc.tensor.transpose(
-                    r_row[:].rearrange("p (q e) -> p q e", e=PACK)[:, :, t],
+                    in_column_order(r_row[:])[:, t // 2, :, t % 2],
                     r[:, t : t + 1].to_broadcast([P, P]),
                     ident_f32[:],
                 )
@@ -118,10 +126,10 @@ def tile_dygcn_pa_t_kernel(tc, A, x, out):
         def regroup_right(b):
             right_grouped = work.tile([P, NODES * PACK], BF16, align_bytes=64)
             right_words = right_grouped[:].rearrange("p (t q s) -> p t q s", t=PACK, s=PACK)
-            columns = live["a_hat", b][:].rearrange("p s (q e) -> p e q s", e=PACK)
+            columns = live["a_hat", b][:].rearrange("p s (u q e) -> p u e q s", u=2, e=2)
             for t in range(PACK):
                 copy = nc.vector.tensor_copy if t < RIGHT_QUARTERS_ON_VECTOR else nc.scalar.copy
-                copy(out=in_runs(right_words[:, t, :, :]), in_=in_runs(columns[:, t, :, :]))
+                copy(out=in_runs(right_words[:, t, :, :]), in_=in_runs(columns[:, t // 2, t % 2, :, :]))
             live["right_grouped", b] = right_grouped
 
         def flip(b):
@@ -130,7 +138,7 @@ def tile_dygcn_pa_t_kernel(tc, A, x, out):
                 for c in range(2):
                     row_words = live["a_hat", b][:, 2 * h + c, :].bitcast(F32)
                     for u in range(2):
-                        nc.tensor.transpose(flipped[:, c, u, :], row_words[:, u : 2 * P : 2], ident_f32[:])
+                        nc.tensor.transpose(flipped[:, c, u, :], row_words[:, u * P : (u + 1) * P], ident_f32[:])
                 live["flipped", b, h] = flipped
 
         def regroup_left(b):
@@ -143,10 +151,14 @@ def tile_dygcn_pa_t_kernel(tc, A, x, out):
             live["left_grouped", b] = left_grouped
 
         def regroup_x(b):
-            x_grouped = work.tile([P, FEATS * PACK], BF16, align_bytes=64)
-            nc.scalar.copy(
+            x_grouped = x_work.tile([P, FEATS * PACK], BF16, align_bytes=64)
+            nc.gpsimd.tensor_scalar(
                 out=in_runs(x_grouped[:].rearrange("p (f s) -> p f s", s=PACK)),
-                in_=in_runs(live["x_raw", b][:].rearrange("p s f -> p f s")),
+                in0=in_runs(live["x_raw", b][:].rearrange("p s f -> p f s")),
+                scalar1=1.0,
+                scalar2=0.0,
+                op0=ALU.mult,
+                op1=ALU.add,
             )
             live["x_grouped", b] = x_grouped
 
@@ -219,6 +231,7 @@ def tile_dygcn_pa_t_kernel(tc, A, x, out):
                 if 0 <= last:
                     times_x(last, "t2")
                 if 0 <= middle < GRAPHS:
+                    regroup_x(middle)
                     scale(middle)
                 if front < GRAPHS:
                     positive_part(front)
@@ -248,8 +261,6 @@ def tile_dygcn_pa_t_kernel(tc, A, x, out):
                     store(back, 0)
                     quantise_as(back, "t2", NODES)
                 if 0 <= middle < GRAPHS:
-                    quantise_as(middle, "x", FEATS)
                     quantise_as(middle, "left", NODES)
                     quantise_as(middle, "right", NODES)
-                if front < GRAPHS:
-                    regroup_x(front)
+                    quantise_as(middle, "x", FEATS)

@@ -17,7 +17,8 @@ FEATS = 256
 P = 128
 PACK = 4
 
-RIGHT_QUARTERS_ON_VECTOR = 2
+RIGHT_ON_GPSIMD = (3,)
+RIGHT_ON_SCALAR = (1, 2)
 LOADS_AHEAD = 4
 
 FLOPS = GRAPHS * 2 * (NODES * NODES * NODES + 2 * NODES * NODES * FEATS)
@@ -35,6 +36,10 @@ def in_runs(view):
     return view.rearrange("p (c i) s -> p c s i", i=4)
 
 
+def relu_on_vector(b):
+    return {0: (1, 3)}.get(b, ())
+
+
 def quantise(nc, pool, grouped, width, name):
     codes = pool.tile([P, width], U32, align_bytes=64, name=name + "_codes")
     scales = pool.tile([P, width], U8, align_bytes=64, name=name + "_scales")
@@ -50,12 +55,17 @@ def tile_dygcn_pa_t_kernel(tc, A, x, out):
         work = stack.enter_context(tc.tile_pool(name="work", bufs=2))
         small = stack.enter_context(tc.tile_pool(name="small", bufs=3))
         mx = stack.enter_context(tc.tile_pool(name="mx", bufs=3))
-        results = stack.enter_context(tc.tile_pool(name="results", bufs=4))
+        results = stack.enter_context(tc.tile_pool(name="results", bufs=8))
         x_work = stack.enter_context(tc.tile_pool(name="x_work", bufs=1))
         ps_row = stack.enter_context(tc.psum_pool(name="ps_row", bufs=1))
         ps_tr = stack.enter_context(tc.psum_pool(name="ps_tr", bufs=2))
         ps_t2 = stack.enter_context(tc.psum_pool(name="ps_t2", bufs=3))
         ps_out = stack.enter_context(tc.psum_pool(name="ps_out", bufs=2))
+
+        one = const.tile([P, 1], F32)
+        nc.vector.memset(one[:], 1.0)
+        root_one = const.tile([P, 1], F32)
+        nc.scalar.activation(out=root_one[:], in_=one[:], func=ACT.Sqrt)
 
         ident_f32 = const.tile([P, P], F32)
         make_identity(nc, ident_f32[:])
@@ -80,19 +90,30 @@ def tile_dygcn_pa_t_kernel(tc, A, x, out):
             pos = work.tile([P, PACK, NODES], F32)
             rowsum = small.tile([P, PACK], F32)
             for t in range(PACK):
-                nc.scalar.activation(
-                    out=in_column_order(pos[:, t, :]),
-                    in_=a_raw[:, t, :].rearrange("p (q u e) -> p u q e", u=2, e=2),
-                    func=ACT.Relu,
-                    accum_out=rowsum[:, t : t + 1],
-                )
-            for t in range(PACK):
-                diag = in_column_order(pos[:, t, :])[:, t // 2, :, t % 2]
-                nc.gpsimd.tensor_tensor(out=diag, in0=diag, in1=ident_f32[:], op=ALU.add)
+                raw = a_raw[:, t, :].rearrange("p (q u e) -> p u q e", u=2, e=2)
+                if t in relu_on_vector(b):
+                    nc.vector.tensor_scalar(
+                        out=in_column_order(pos[:, t, :]),
+                        in0=raw,
+                        scalar1=0.0,
+                        scalar2=None,
+                        op0=ALU.max,
+                        op1=ALU.add,
+                        accum_out=rowsum[:, t : t + 1],
+                    )
+                else:
+                    nc.scalar.activation(
+                        out=in_column_order(pos[:, t, :]), in_=raw, func=ACT.Relu, accum_out=rowsum[:, t : t + 1]
+                    )
             root_deg = small.tile([P, PACK], F32)
             nc.scalar.activation(out=root_deg[:], in_=rowsum[:], func=ACT.Sqrt, bias=1.0)
             live["pos", b] = pos
             live["root_deg", b] = root_deg
+
+        def add_identity(b):
+            for t in range(PACK):
+                diag = in_column_order(live["pos", b][:, t, :])[:, t // 2, :, t % 2]
+                nc.gpsimd.tensor_tensor(out=diag, in0=diag, in1=ident_f32[:], op=ALU.add)
 
         def inverse_root(b):
             r = small.tile([P, PACK], F32)
@@ -110,51 +131,62 @@ def tile_dygcn_pa_t_kernel(tc, A, x, out):
                 )
             live["r_row", b] = r_row
 
-        def scale(b):
-            a_hat = work.tile([P, PACK, NODES], BF16)
-            for t in range(PACK):
+        def scale(b, slots=range(PACK)):
+            if 0 in slots:
+                live["a_hat", b] = work.tile([P, PACK, NODES], BF16, name="a_hat")
+            for t in slots:
                 nc.vector.scalar_tensor_tensor(
-                    out=a_hat[:, t, :],
+                    out=live["a_hat", b][:, t, :],
                     in0=live["pos", b][:, t, :],
                     scalar=live["r", b][:, t : t + 1],
                     in1=live["r_row", b][:],
                     op0=ALU.mult,
                     op1=ALU.mult,
                 )
-            live["a_hat", b] = a_hat
 
-        def regroup_right(b):
-            right_grouped = work.tile([P, NODES * PACK], BF16, align_bytes=64)
-            right_words = right_grouped[:].rearrange("p (t q s) -> p t q s", t=PACK, s=PACK)
-            columns = live["a_hat", b][:].rearrange("p s (u q e) -> p u e q s", u=2, e=2)
-            for t in range(PACK):
-                copy = nc.vector.tensor_copy if t < RIGHT_QUARTERS_ON_VECTOR else nc.scalar.copy
-                copy(out=in_runs(right_words[:, t, :, :]), in_=in_runs(columns[:, t // 2, t % 2, :, :]))
-            live["right_grouped", b] = right_grouped
+        def right_columns(b, t):
+            return live["a_hat", b][:].rearrange("p s (u q e) -> p u e q s", u=2, e=2)[:, t // 2, t % 2, :, :]
 
-        def flip(b):
-            for h in range(2):
-                flipped = ps_tr.tile([P, 2, 2, P], F32)
-                for c in range(2):
-                    row_words = live["a_hat", b][:, 2 * h + c, :].bitcast(F32)
-                    for u in range(2):
-                        nc.tensor.transpose(flipped[:, c, u, :], row_words[:, u * P : (u + 1) * P], ident_f32[:])
-                live["flipped", b, h] = flipped
+        def regroup_right(b, quarters):
+            if 0 in quarters:
+                live["right_grouped", b] = work.tile([P, NODES * PACK], BF16, align_bytes=64, name="right_grouped")
+            right_words = live["right_grouped", b][:].rearrange("p (t q s) -> p t q s", t=PACK, s=PACK)
+            for t in quarters:
+                grouped, columns = right_words[:, t, :, :], right_columns(b, t)
+                if t not in RIGHT_ON_GPSIMD or b == 0:
+                    grouped, columns = in_runs(grouped), in_runs(columns)
+                if b == 0:
+                    nc.vector.tensor_copy(out=grouped, in_=columns)
+                elif t in RIGHT_ON_GPSIMD:
+                    nc.gpsimd.tensor_scalar(
+                        out=grouped, in0=columns, scalar1=1.0, scalar2=0.0, op0=ALU.mult, op1=ALU.add
+                    )
+                elif t in RIGHT_ON_SCALAR:
+                    nc.scalar.copy(out=grouped, in_=columns)
+                else:
+                    nc.vector.tensor_copy(out=grouped, in_=columns)
 
-        def regroup_left(b):
-            left_grouped = work.tile([P, NODES * PACK], BF16, align_bytes=64)
-            left_words = left_grouped[:].bitcast(F32).rearrange("p (h c n u) -> p h c n u", h=2, c=2, u=2)
-            for h in range(2):
-                nc.scalar.copy(
-                    out=left_words[:, h, :, :, :], in_=live["flipped", b, h][:].rearrange("p c u n -> p c n u")
-                )
-            live["left_grouped", b] = left_grouped
+        def flip(b, h):
+            flipped = ps_tr.tile([P, 2, 2, P], F32)
+            for c in range(2):
+                row_words = live["a_hat", b][:, 2 * h + c, :].bitcast(F32)
+                for u in range(2):
+                    nc.tensor.transpose(flipped[:, c, u, :], row_words[:, u * P : (u + 1) * P], ident_f32[:])
+            live["flipped", b, h] = flipped
+
+        def regroup_left(b, h):
+            if h == 0:
+                live["left_grouped", b] = work.tile([P, NODES * PACK], BF16, align_bytes=64, name="left_grouped")
+            left_words = live["left_grouped", b][:].bitcast(F32).rearrange("p (h c n u) -> p h c n u", h=2, c=2, u=2)
+            nc.scalar.copy(
+                out=left_words[:, h, :, :, :], in_=live["flipped", b, h][:].rearrange("p c u n -> p c n u")
+            )
 
         def regroup_x(b):
             x_grouped = x_work.tile([P, FEATS * PACK], BF16, align_bytes=64)
             nc.gpsimd.tensor_scalar(
-                out=in_runs(x_grouped[:].rearrange("p (f s) -> p f s", s=PACK)),
-                in0=in_runs(live["x_raw", b][:].rearrange("p s f -> p f s")),
+                out=x_grouped[:].rearrange("p (f s) -> p f s", s=PACK),
+                in0=live["x_raw", b][:].rearrange("p s f -> p f s"),
                 scalar1=1.0,
                 scalar2=0.0,
                 op0=ALU.mult,
@@ -210,13 +242,11 @@ def tile_dygcn_pa_t_kernel(tc, A, x, out):
                     )
                 live["acc", b, h] = acc
 
-        def store(b, which):
-            result = results.tile([P, PACK, FEATS], F32)
-            for h in range(2):
-                nc.scalar.copy(out=result[:, 2 * h : 2 * h + 2, :], in_=live["acc", b, h][:])
-                nc.sync.dma_start(
-                    out=rows_by_node(out[b, which])[:, 2 * h : 2 * h + 2, :], in_=result[:, 2 * h : 2 * h + 2, :]
-                )
+        def store(b, which, h):
+            result = results.tile([P, 2, FEATS], F32)
+            copy = nc.vector.tensor_copy if b == GRAPHS - 1 and h == 1 else nc.scalar.copy
+            copy(out=result[:], in_=live["acc", b, h][:])
+            nc.sync.dma_start(out=rows_by_node(out[b, which])[:, 2 * h : 2 * h + 2, :], in_=result[:])
 
         def quantise_as(b, name, width):
             live[name, b] = quantise(nc, mx, live[name + "_grouped", b][:], width, name)
@@ -235,20 +265,26 @@ def tile_dygcn_pa_t_kernel(tc, A, x, out):
                     scale(middle)
                 if front < GRAPHS:
                     positive_part(front)
+                    add_identity(front)
                 if 0 <= back < GRAPHS:
-                    for c in range(PACK - 1):
-                        square(back, c)
+                    square(back, 0)
+                    square(back, 1)
+                    square(back, 2)
                 if 0 <= last:
-                    store(last, 1)
+                    store(last, 1, 0)
+                    store(last, 1, 1)
                 if 0 <= middle < GRAPHS:
-                    flip(middle)
+                    flip(middle, 0)
+                    flip(middle, 1)
                 if 0 <= back < GRAPHS:
-                    for c in range(PACK - 1):
-                        chebyshev(back, c)
-                    square(back, PACK - 1)
-                    chebyshev(back, PACK - 1)
+                    chebyshev(back, 0)
+                    chebyshev(back, 1)
+                    chebyshev(back, 2)
+                    square(back, 3)
+                    chebyshev(back, 3)
                 if 0 <= middle < GRAPHS:
-                    regroup_left(middle)
+                    regroup_left(middle, 0)
+                    regroup_left(middle, 1)
                 if front < GRAPHS:
                     inverse_root(front)
                 if 0 <= back < GRAPHS:
@@ -256,9 +292,10 @@ def tile_dygcn_pa_t_kernel(tc, A, x, out):
                 if front < GRAPHS:
                     spread_r(front)
                 if 0 <= middle < GRAPHS:
-                    regroup_right(middle)
+                    regroup_right(middle, (0, 1, 2, 3))
                 if 0 <= back < GRAPHS:
-                    store(back, 0)
+                    store(back, 0, 0)
+                    store(back, 0, 1)
                     quantise_as(back, "t2", NODES)
                 if 0 <= middle < GRAPHS:
                     quantise_as(middle, "left", NODES)

@@ -17,8 +17,7 @@ FEATS = 256
 P = 128
 PACK = 4
 
-RIGHT_ON_GPSIMD = (3,)
-RIGHT_ON_SCALAR = (1, 2)
+RIGHT_ON_SCALAR = (2, 3)
 LOADS_AHEAD = 4
 
 FLOPS = GRAPHS * 2 * (NODES * NODES * NODES + 2 * NODES * NODES * FEATS)
@@ -40,21 +39,14 @@ def relu_on_vector(b):
     return {0: (1, 3)}.get(b, ())
 
 
-def quantise(nc, pool, grouped, width, name):
-    codes = pool.tile([P, width], U32, align_bytes=64, name=name + "_codes")
-    scales = pool.tile([P, width], U8, align_bytes=64, name=name + "_scales")
-    nc.vector.quantize_mx(out=codes[:].bitcast(FP8X4), scales=scales[:], in_=grouped)
-    return codes, scales
-
-
 def tile_dygcn_pa_t_kernel(tc, A, x, out):
     nc = tc.nc
     with ExitStack() as stack:
         const = stack.enter_context(tc.tile_pool(name="const", bufs=1))
         loads = stack.enter_context(tc.tile_pool(name="loads", bufs=LOADS_AHEAD + 2))
-        work = stack.enter_context(tc.tile_pool(name="work", bufs=2))
-        small = stack.enter_context(tc.tile_pool(name="small", bufs=3))
-        mx = stack.enter_context(tc.tile_pool(name="mx", bufs=3))
+        work = stack.enter_context(tc.tile_pool(name="work", bufs=3))
+        small = stack.enter_context(tc.tile_pool(name="small", bufs=4))
+        mx = stack.enter_context(tc.tile_pool(name="mx", bufs=4))
         results = stack.enter_context(tc.tile_pool(name="results", bufs=8))
         x_work = stack.enter_context(tc.tile_pool(name="x_work", bufs=1))
         ps_row = stack.enter_context(tc.psum_pool(name="ps_row", bufs=1))
@@ -72,7 +64,9 @@ def tile_dygcn_pa_t_kernel(tc, A, x, out):
         eye_t2 = const.tile([P, PACK, P, PACK], BF16)
         nc.vector.memset(eye_t2[:], 0.0)
         for c in range(PACK):
-            nc.vector.tensor_copy(out=eye_t2[:, c, :, c], in_=ident_f32[:])
+            nc.gpsimd.tensor_scalar(
+                out=eye_t2[:, c, :, c], in0=ident_f32[:], scalar1=1.0, scalar2=0.0, op0=ALU.mult, op1=ALU.add
+            )
 
         live = {}
 
@@ -152,19 +146,8 @@ def tile_dygcn_pa_t_kernel(tc, A, x, out):
                 live["right_grouped", b] = work.tile([P, NODES * PACK], BF16, align_bytes=64, name="right_grouped")
             right_words = live["right_grouped", b][:].rearrange("p (t q s) -> p t q s", t=PACK, s=PACK)
             for t in quarters:
-                grouped, columns = right_words[:, t, :, :], right_columns(b, t)
-                if t not in RIGHT_ON_GPSIMD or b == 0:
-                    grouped, columns = in_runs(grouped), in_runs(columns)
-                if b == 0:
-                    nc.vector.tensor_copy(out=grouped, in_=columns)
-                elif t in RIGHT_ON_GPSIMD:
-                    nc.gpsimd.tensor_scalar(
-                        out=grouped, in0=columns, scalar1=1.0, scalar2=0.0, op0=ALU.mult, op1=ALU.add
-                    )
-                elif t in RIGHT_ON_SCALAR:
-                    nc.scalar.copy(out=grouped, in_=columns)
-                else:
-                    nc.vector.tensor_copy(out=grouped, in_=columns)
+                copy = nc.scalar.copy if t in RIGHT_ON_SCALAR and b > 0 else nc.vector.tensor_copy
+                copy(out=in_runs(right_words[:, t, :, :]), in_=in_runs(right_columns(b, t)))
 
         def flip(b, h):
             flipped = ps_tr.tile([P, 2, 2, P], F32)
@@ -185,8 +168,8 @@ def tile_dygcn_pa_t_kernel(tc, A, x, out):
         def regroup_x(b):
             x_grouped = x_work.tile([P, FEATS * PACK], BF16, align_bytes=64)
             nc.gpsimd.tensor_scalar(
-                out=x_grouped[:].rearrange("p (f s) -> p f s", s=PACK),
-                in0=live["x_raw", b][:].rearrange("p s f -> p f s"),
+                out=in_runs(x_grouped[:].rearrange("p (f s) -> p f s", s=PACK)),
+                in0=in_runs(live["x_raw", b][:].rearrange("p s f -> p f s")),
                 scalar1=1.0,
                 scalar2=0.0,
                 op0=ALU.mult,
@@ -244,12 +227,22 @@ def tile_dygcn_pa_t_kernel(tc, A, x, out):
 
         def store(b, which, h):
             result = results.tile([P, 2, FEATS], F32)
-            copy = nc.vector.tensor_copy if b == GRAPHS - 1 and h == 1 else nc.scalar.copy
+            copy = nc.vector.tensor_copy if (b, which, h) == (GRAPHS - 1, 1, 1) else nc.scalar.copy
             copy(out=result[:], in_=live["acc", b, h][:])
             nc.sync.dma_start(out=rows_by_node(out[b, which])[:, 2 * h : 2 * h + 2, :], in_=result[:])
 
-        def quantise_as(b, name, width):
-            live[name, b] = quantise(nc, mx, live[name + "_grouped", b][:], width, name)
+        def quantise(b, name, width, begin=0, end=None):
+            end = width if end is None else end
+            if begin == 0:
+                codes = mx.tile([P, width], U32, align_bytes=64, name=name + "_codes")
+                scales = mx.tile([P, width], U8, align_bytes=64, name=name + "_scales")
+                live[name, b] = codes, scales
+            codes, scales = live[name, b]
+            nc.vector.quantize_mx(
+                out=codes[:, begin:end].bitcast(FP8X4),
+                scales=scales[:, begin:end],
+                in_=live[name + "_grouped", b][:, begin * PACK : end * PACK],
+            )
 
         with tc.manual_schedule():
             for b in range(LOADS_AHEAD):
@@ -280,6 +273,8 @@ def tile_dygcn_pa_t_kernel(tc, A, x, out):
                     chebyshev(back, 0)
                     chebyshev(back, 1)
                     chebyshev(back, 2)
+                    if back == GRAPHS - 1:
+                        quantise(back, "t2", NODES, 0, NODES // 2)
                     square(back, 3)
                     chebyshev(back, 3)
                 if 0 <= middle < GRAPHS:
@@ -296,8 +291,8 @@ def tile_dygcn_pa_t_kernel(tc, A, x, out):
                 if 0 <= back < GRAPHS:
                     store(back, 0, 0)
                     store(back, 0, 1)
-                    quantise_as(back, "t2", NODES)
+                    quantise(back, "t2", NODES, NODES // 2 if back == GRAPHS - 1 else 0)
                 if 0 <= middle < GRAPHS:
-                    quantise_as(middle, "left", NODES)
-                    quantise_as(middle, "right", NODES)
-                    quantise_as(middle, "x", FEATS)
+                    quantise(middle, "left", NODES)
+                    quantise(middle, "right", NODES)
+                    quantise(middle, "x", FEATS)

@@ -17,7 +17,8 @@ FEATS = 256
 P = 128
 PACK = 4
 
-RIGHT_ON_SCALAR = (2, 3)
+RIGHT_ON_SCALAR = (1, 2)
+RIGHT_ON_GPSIMD = (3,)
 LOADS_AHEAD = 4
 
 FLOPS = GRAPHS * 2 * (NODES * NODES * NODES + 2 * NODES * NODES * FEATS)
@@ -104,8 +105,8 @@ def tile_dygcn_pa_t_kernel(tc, A, x, out):
             live["pos", b] = pos
             live["root_deg", b] = root_deg
 
-        def add_identity(b):
-            for t in range(PACK):
+        def add_identity(b, slots):
+            for t in slots:
                 diag = in_column_order(live["pos", b][:, t, :])[:, t // 2, :, t % 2]
                 nc.gpsimd.tensor_tensor(out=diag, in0=diag, in1=ident_f32[:], op=ALU.add)
 
@@ -142,12 +143,23 @@ def tile_dygcn_pa_t_kernel(tc, A, x, out):
             return live["a_hat", b][:].rearrange("p s (u q e) -> p u e q s", u=2, e=2)[:, t // 2, t % 2, :, :]
 
         def regroup_right(b, quarters):
-            if 0 in quarters:
+            if ("right_grouped", b) not in live:
                 live["right_grouped", b] = work.tile([P, NODES * PACK], BF16, align_bytes=64, name="right_grouped")
             right_words = live["right_grouped", b][:].rearrange("p (t q s) -> p t q s", t=PACK, s=PACK)
             for t in quarters:
-                copy = nc.scalar.copy if t in RIGHT_ON_SCALAR and b > 0 else nc.vector.tensor_copy
-                copy(out=in_runs(right_words[:, t, :, :]), in_=in_runs(right_columns(b, t)))
+                grouped, columns = right_words[:, t, :, :], right_columns(b, t)
+                if t in RIGHT_ON_GPSIMD and b > 0:
+                    nc.gpsimd.tensor_scalar(
+                        out=in_runs(grouped),
+                        in0=in_runs(columns),
+                        scalar1=1.0,
+                        scalar2=0.0,
+                        op0=ALU.mult,
+                        op1=ALU.add,
+                    )
+                else:
+                    copy = nc.scalar.copy if t in RIGHT_ON_SCALAR and b > 0 else nc.vector.tensor_copy
+                    copy(out=in_runs(grouped), in_=in_runs(columns))
 
         def flip(b, h):
             flipped = ps_tr.tile([P, 2, 2, P], F32)
@@ -258,7 +270,11 @@ def tile_dygcn_pa_t_kernel(tc, A, x, out):
                     scale(middle)
                 if front < GRAPHS:
                     positive_part(front)
-                    add_identity(front)
+                    add_identity(front, (0, 1))
+                if 0 <= middle < GRAPHS:
+                    regroup_right(middle, (3,))
+                if front < GRAPHS:
+                    add_identity(front, (2, 3))
                 if 0 <= back < GRAPHS:
                     square(back, 0)
                     square(back, 1)
@@ -287,7 +303,7 @@ def tile_dygcn_pa_t_kernel(tc, A, x, out):
                 if front < GRAPHS:
                     spread_r(front)
                 if 0 <= middle < GRAPHS:
-                    regroup_right(middle, (0, 1, 2, 3))
+                    regroup_right(middle, (0, 1, 2))
                 if 0 <= back < GRAPHS:
                     store(back, 0, 0)
                     store(back, 0, 1)

@@ -62,6 +62,11 @@ def tile_dygcn_pa_t_kernel(tc, A, x, out):
 
         ident_f32 = const.tile([P, P], F32)
         make_identity(nc, ident_f32[:])
+        ident_x4 = const.tile([P, 2, 2, P], F32)
+        for t in range(PACK):
+            nc.gpsimd.tensor_scalar(
+                out=ident_x4[:, t // 2, t % 2, :], in0=ident_f32[:], scalar1=1.0, scalar2=0.0, op0=ALU.mult, op1=ALU.add
+            )
         eye_t2 = const.tile([P, PACK, P, PACK], BF16)
         nc.vector.memset(eye_t2[:], 0.0)
         for c in range(PACK):
@@ -82,13 +87,14 @@ def tile_dygcn_pa_t_kernel(tc, A, x, out):
 
         def positive_part(b):
             a_raw = live["a_raw", b]
-            pos = work.tile([P, PACK, NODES], F32)
+            pos = work.tile([P, 18, P], F32)
             rowsum = small.tile([P, PACK], F32)
             for t in range(PACK):
-                raw = a_raw[:, t, :].rearrange("p (q u e) -> p u q e", u=2, e=2)
+                raw = a_raw[:, t, :].rearrange("p (q u e) -> p e u q", u=2, e=2)
+                pos_row = pos[:, 4 * t : 4 * t + 4, :].rearrange("p (e u) q -> p e u q", e=2)
                 if t in relu_on_vector(b):
                     nc.vector.tensor_scalar(
-                        out=in_column_order(pos[:, t, :]),
+                        out=pos_row,
                         in0=raw,
                         scalar1=0.0,
                         scalar2=None,
@@ -98,17 +104,16 @@ def tile_dygcn_pa_t_kernel(tc, A, x, out):
                     )
                 else:
                     nc.scalar.activation(
-                        out=in_column_order(pos[:, t, :]), in_=raw, func=ACT.Relu, accum_out=rowsum[:, t : t + 1]
+                        out=pos_row, in_=raw, func=ACT.Relu, accum_out=rowsum[:, t : t + 1]
                     )
             root_deg = small.tile([P, PACK], F32)
             nc.scalar.activation(out=root_deg[:], in_=rowsum[:], func=ACT.Sqrt, bias=1.0)
             live["pos", b] = pos
             live["root_deg", b] = root_deg
 
-        def add_identity(b, slots):
-            for t in slots:
-                diag = in_column_order(live["pos", b][:, t, :])[:, t // 2, :, t % 2]
-                nc.gpsimd.tensor_tensor(out=diag, in0=diag, in1=ident_f32[:], op=ALU.add)
+        def add_identity(b):
+            diag = live["pos", b][:].rearrange("p (u k) q -> p u k q", u=2)[:, :, 0:7:6, :]
+            nc.gpsimd.tensor_tensor(out=diag, in0=diag, in1=ident_x4[:], op=ALU.add)
 
         def inverse_root(b):
             r = small.tile([P, PACK], F32)
@@ -131,10 +136,10 @@ def tile_dygcn_pa_t_kernel(tc, A, x, out):
                 live["a_hat", b] = work.tile([P, PACK, NODES], BF16, name="a_hat")
             for t in slots:
                 nc.vector.scalar_tensor_tensor(
-                    out=live["a_hat", b][:, t, :],
-                    in0=live["pos", b][:, t, :],
+                    out=live["a_hat", b][:, t, :].rearrange("p (w e) -> p w e", e=2),
+                    in0=live["pos", b][:, 4 * t : 4 * t + 4, :].rearrange("p (e u) q -> p (u q) e", e=2),
                     scalar=live["r", b][:, t : t + 1],
-                    in1=live["r_row", b][:],
+                    in1=live["r_row", b][:].rearrange("p (w e) -> p w e", e=2),
                     op0=ALU.mult,
                     op1=ALU.mult,
                 )
@@ -270,11 +275,9 @@ def tile_dygcn_pa_t_kernel(tc, A, x, out):
                     scale(middle)
                 if front < GRAPHS:
                     positive_part(front)
-                    add_identity(front, (0, 1))
+                    add_identity(front)
                 if 0 <= middle < GRAPHS:
                     regroup_right(middle, (3,))
-                if front < GRAPHS:
-                    add_identity(front, (2, 3))
                 if 0 <= back < GRAPHS:
                     square(back, 0)
                     square(back, 1)

@@ -17,8 +17,6 @@ FEATS = 256
 P = 128
 PACK = 4
 
-RIGHT_ON_SCALAR = (1, 2)
-RIGHT_ON_GPSIMD = (3,)
 LOADS_AHEAD = 4
 
 FLOPS = GRAPHS * 2 * (NODES * NODES * NODES + 2 * NODES * NODES * FEATS)
@@ -62,11 +60,9 @@ def tile_dygcn_pa_t_kernel(tc, A, x, out):
 
         ident_f32 = const.tile([P, P], F32)
         make_identity(nc, ident_f32[:])
-        ident_x4 = const.tile([P, 2, 2, P], F32)
-        for t in range(PACK):
-            nc.gpsimd.tensor_scalar(
-                out=ident_x4[:, t // 2, t % 2, :], in0=ident_f32[:], scalar1=1.0, scalar2=0.0, op0=ALU.mult, op1=ALU.add
-            )
+        ident_x2 = const.tile([P, 2, P], F32)
+        for e in range(2):
+            nc.vector.tensor_copy(out=ident_x2[:, e, :], in_=ident_f32[:])
         eye_t2 = const.tile([P, PACK, P, PACK], BF16)
         nc.vector.memset(eye_t2[:], 0.0)
         for c in range(PACK):
@@ -87,7 +83,7 @@ def tile_dygcn_pa_t_kernel(tc, A, x, out):
 
         def positive_part(b):
             a_raw = live["a_raw", b]
-            pos = work.tile([P, 18, P], F32)
+            pos = work.tile([P, 4 * PACK, P], F32)
             rowsum = small.tile([P, PACK], F32)
             for t in range(PACK):
                 raw = a_raw[:, t, :].rearrange("p (q u e) -> p e u q", u=2, e=2)
@@ -106,14 +102,17 @@ def tile_dygcn_pa_t_kernel(tc, A, x, out):
                     nc.scalar.activation(
                         out=pos_row, in_=raw, func=ACT.Relu, accum_out=rowsum[:, t : t + 1]
                     )
-            root_deg = small.tile([P, PACK], F32)
-            nc.scalar.activation(out=root_deg[:], in_=rowsum[:], func=ACT.Sqrt, bias=1.0)
             live["pos", b] = pos
+            live["rowsum", b] = rowsum
+
+        def root_degree(b):
+            root_deg = small.tile([P, PACK], F32)
+            nc.scalar.activation(out=root_deg[:], in_=live["rowsum", b][:], func=ACT.Sqrt, bias=1.0)
             live["root_deg", b] = root_deg
 
-        def add_identity(b):
-            diag = live["pos", b][:].rearrange("p (u k) q -> p u k q", u=2)[:, :, 0:7:6, :]
-            nc.gpsimd.tensor_tensor(out=diag, in0=diag, in1=ident_x4[:], op=ALU.add)
+        def add_identity(b, u):
+            diag = live["pos", b][:, 9 * u : 9 * u + 7 : 6, :]
+            nc.gpsimd.tensor_tensor(out=diag, in0=diag, in1=ident_x2[:], op=ALU.add)
 
         def inverse_root(b):
             r = small.tile([P, PACK], F32)
@@ -144,27 +143,24 @@ def tile_dygcn_pa_t_kernel(tc, A, x, out):
                     op1=ALU.mult,
                 )
 
-        def right_columns(b, t):
-            return live["a_hat", b][:].rearrange("p s (u q e) -> p u e q s", u=2, e=2)[:, t // 2, t % 2, :, :]
-
-        def regroup_right(b, quarters):
+        def regroup_right(b, e):
             if ("right_grouped", b) not in live:
                 live["right_grouped", b] = work.tile([P, NODES * PACK], BF16, align_bytes=64, name="right_grouped")
-            right_words = live["right_grouped", b][:].rearrange("p (t q s) -> p t q s", t=PACK, s=PACK)
-            for t in quarters:
-                grouped, columns = right_words[:, t, :, :], right_columns(b, t)
-                if t in RIGHT_ON_GPSIMD and b > 0:
-                    nc.gpsimd.tensor_scalar(
-                        out=in_runs(grouped),
-                        in0=in_runs(columns),
-                        scalar1=1.0,
-                        scalar2=0.0,
-                        op0=ALU.mult,
-                        op1=ALU.add,
-                    )
-                else:
-                    copy = nc.scalar.copy if t in RIGHT_ON_SCALAR and b > 0 else nc.vector.tensor_copy
-                    copy(out=in_runs(grouped), in_=in_runs(columns))
+            grouped = live["right_grouped", b][:].rearrange("p (e w s) -> p e w s", e=2, s=PACK)[:, e, :, :]
+            columns = live["a_hat", b][:].rearrange("p s (w e) -> p e w s", e=2)[:, e, :, :]
+            if b == 0:
+                nc.vector.tensor_copy(out=in_runs(grouped), in_=in_runs(columns))
+            elif e == 0:
+                nc.scalar.copy(out=in_runs(grouped), in_=in_runs(columns))
+            else:
+                nc.gpsimd.tensor_scalar(
+                    out=in_runs(grouped),
+                    in0=in_runs(columns),
+                    scalar1=1.0,
+                    scalar2=0.0,
+                    op0=ALU.mult,
+                    op1=ALU.add,
+                )
 
         def flip(b, h):
             flipped = ps_tr.tile([P, 2, 2, P], F32)
@@ -200,7 +196,8 @@ def tile_dygcn_pa_t_kernel(tc, A, x, out):
             n_cols = slice(c * P, (c + 1) * P)
             squared = ps_t2.tile([P, PACK, P], F32)
             for t in range(PACK):
-                j_cols = slice(t * P, (t + 1) * P)
+                block = 2 * (t % 2) + t // 2
+                j_cols = slice(block * P, (block + 1) * P)
                 nc.tensor.matmul_mx(
                     out=squared[:, t, :],
                     lhsT=right_codes[:, j_cols].bitcast(FP8X4),
@@ -275,15 +272,20 @@ def tile_dygcn_pa_t_kernel(tc, A, x, out):
                     scale(middle)
                 if front < GRAPHS:
                     positive_part(front)
-                    add_identity(front)
+                    add_identity(front, 0)
                 if 0 <= middle < GRAPHS:
-                    regroup_right(middle, (3,))
+                    regroup_right(middle, 1)
+                if front < GRAPHS:
+                    add_identity(front, 1)
                 if 0 <= back < GRAPHS:
                     square(back, 0)
                     square(back, 1)
                     square(back, 2)
                 if 0 <= last:
                     store(last, 1, 0)
+                if front < GRAPHS:
+                    root_degree(front)
+                if 0 <= last:
                     store(last, 1, 1)
                 if 0 <= middle < GRAPHS:
                     flip(middle, 0)
@@ -306,12 +308,14 @@ def tile_dygcn_pa_t_kernel(tc, A, x, out):
                 if front < GRAPHS:
                     spread_r(front)
                 if 0 <= middle < GRAPHS:
-                    regroup_right(middle, (0, 1, 2))
+                    regroup_right(middle, 0)
                 if 0 <= back < GRAPHS:
                     store(back, 0, 0)
                     store(back, 0, 1)
-                    quantise(back, "t2", NODES, NODES // 2 if back == GRAPHS - 1 else 0)
                 if 0 <= middle < GRAPHS:
                     quantise(middle, "left", NODES)
+                if 0 <= back < GRAPHS:
+                    quantise(back, "t2", NODES, NODES // 2 if back == GRAPHS - 1 else 0)
+                if 0 <= middle < GRAPHS:
                     quantise(middle, "right", NODES)
                     quantise(middle, "x", FEATS)

@@ -56,7 +56,7 @@ def tile_dygcn_pa_t_kernel(tc, A, x, out):
         one = const.tile([P, 1], F32)
         nc.vector.memset(one[:], 1.0)
         root_one = const.tile([P, 1], F32)
-        nc.scalar.activation(out=root_one[:], in_=one[:], func=ACT.Sqrt)
+        nc.scalar.activation(out=root_one[:], in_=one[:], func=ACT.Abs_reciprocal_sqrt)
 
         ident_f32 = const.tile([P, P], F32)
         make_identity(nc, ident_f32[:])
@@ -105,10 +105,6 @@ def tile_dygcn_pa_t_kernel(tc, A, x, out):
             live["pos", b] = pos
             live["rowsum", b] = rowsum
 
-        def root_degree(b):
-            root_deg = small.tile([P, PACK], F32)
-            nc.scalar.activation(out=root_deg[:], in_=live["rowsum", b][:], func=ACT.Sqrt, bias=1.0)
-            live["root_deg", b] = root_deg
 
         def add_identity(b, u):
             diag = live["pos", b][:, 9 * u : 9 * u + 7 : 6, :]
@@ -116,7 +112,7 @@ def tile_dygcn_pa_t_kernel(tc, A, x, out):
 
         def inverse_root(b):
             r = small.tile([P, PACK], F32)
-            nc.vector.reciprocal(out=r[:], in_=live["root_deg", b][:])
+            nc.scalar.activation(out=r[:], in_=live["rowsum", b][:], func=ACT.Abs_reciprocal_sqrt, bias=1.0)
             live["r", b] = r
 
         def spread_r(b):
@@ -149,14 +145,16 @@ def tile_dygcn_pa_t_kernel(tc, A, x, out):
             grouped = live["right_grouped", b][:].rearrange("p (e w s) -> p e w s", e=2, s=PACK)[:, e, :, :]
             columns = live["a_hat", b][:].rearrange("p s (w e) -> p e w s", e=2)[:, e, :, :]
             if b == 0:
-                nc.vector.tensor_copy(out=in_runs(grouped), in_=in_runs(columns))
+                nc.vector.tensor_scalar(
+                    out=in_runs(grouped), in0=in_runs(columns), scalar1=2.0, scalar2=None, op0=ALU.mult
+                )
             elif e == 0:
-                nc.scalar.copy(out=in_runs(grouped), in_=in_runs(columns))
+                nc.scalar.activation(out=in_runs(grouped), in_=in_runs(columns), func=ACT.Copy, scale=2.0)
             else:
                 nc.gpsimd.tensor_scalar(
                     out=in_runs(grouped),
                     in0=in_runs(columns),
-                    scalar1=1.0,
+                    scalar1=2.0,
                     scalar2=0.0,
                     op0=ALU.mult,
                     op1=ALU.add,
@@ -212,13 +210,11 @@ def tile_dygcn_pa_t_kernel(tc, A, x, out):
         def chebyshev(b, c):
             if c == 0:
                 live["t2_grouped", b] = work.tile([P, NODES * PACK], BF16, align_bytes=64, name="t2_grouped")
-            nc.vector.scalar_tensor_tensor(
+            nc.vector.tensor_tensor(
                 out=live["t2_grouped", b][:].rearrange("p (c n t) -> p c n t", c=PACK, t=PACK)[:, c, :, :],
                 in0=live["squared", b, c][:].rearrange("p t n -> p n t"),
-                scalar=2.0,
                 in1=eye_t2[:, c, :, :],
-                op0=ALU.mult,
-                op1=ALU.subtract,
+                op=ALU.subtract,
             )
 
         def times_x(b, name):
@@ -284,7 +280,7 @@ def tile_dygcn_pa_t_kernel(tc, A, x, out):
                 if 0 <= last:
                     store(last, 1, 0)
                 if front < GRAPHS:
-                    root_degree(front)
+                    inverse_root(front)
                 if 0 <= last:
                     store(last, 1, 1)
                 if 0 <= middle < GRAPHS:
@@ -301,8 +297,6 @@ def tile_dygcn_pa_t_kernel(tc, A, x, out):
                 if 0 <= middle < GRAPHS:
                     regroup_left(middle, 0)
                     regroup_left(middle, 1)
-                if front < GRAPHS:
-                    inverse_root(front)
                 if 0 <= back < GRAPHS:
                     times_x(back, "left")
                 if front < GRAPHS:

@@ -17,6 +17,7 @@ FEATS = 256
 P = 128
 PACK = 4
 
+SCALAR_RUNS = 56
 LOADS_AHEAD = 4
 
 FLOPS = GRAPHS * 2 * (NODES * NODES * NODES + 2 * NODES * NODES * FEATS)
@@ -63,11 +64,11 @@ def tile_dygcn_pa_t_kernel(tc, A, x, out):
         ident_x2 = const.tile([P, 2, P], F32)
         for e in range(2):
             nc.vector.tensor_copy(out=ident_x2[:, e, :], in_=ident_f32[:])
-        eye_t2 = const.tile([P, PACK, P, PACK], BF16)
-        nc.vector.memset(eye_t2[:], 0.0)
+        half_eye = const.tile([P, PACK, P, PACK], BF16)
+        nc.vector.memset(half_eye[:], 0.0)
         for c in range(PACK):
             nc.gpsimd.tensor_scalar(
-                out=eye_t2[:, c, :, c], in0=ident_f32[:], scalar1=1.0, scalar2=0.0, op0=ALU.mult, op1=ALU.add
+                out=half_eye[:, c, :, c], in0=ident_f32[:], scalar1=0.5, scalar2=0.0, op0=ALU.mult, op1=ALU.add
             )
 
         live = {}
@@ -144,17 +145,17 @@ def tile_dygcn_pa_t_kernel(tc, A, x, out):
                 live["right_grouped", b] = work.tile([P, NODES * PACK], BF16, align_bytes=64, name="right_grouped")
             grouped = live["right_grouped", b][:].rearrange("p (e w s) -> p e w s", e=2, s=PACK)[:, e, :, :]
             columns = live["a_hat", b][:].rearrange("p s (w e) -> p e w s", e=2)[:, e, :, :]
+            to, source = in_runs(grouped), in_runs(columns)
             if b == 0:
-                nc.vector.tensor_scalar(
-                    out=in_runs(grouped), in0=in_runs(columns), scalar1=2.0, scalar2=None, op0=ALU.mult
-                )
+                nc.vector.tensor_copy(out=to, in_=source)
             elif e == 0:
-                nc.scalar.activation(out=in_runs(grouped), in_=in_runs(columns), func=ACT.Copy, scale=2.0)
+                nc.scalar.copy(out=to[:, :SCALAR_RUNS], in_=source[:, :SCALAR_RUNS])
+                nc.vector.tensor_copy(out=to[:, SCALAR_RUNS:], in_=source[:, SCALAR_RUNS:])
             else:
                 nc.gpsimd.tensor_scalar(
-                    out=in_runs(grouped),
-                    in0=in_runs(columns),
-                    scalar1=2.0,
+                    out=to,
+                    in0=source,
+                    scalar1=1.0,
                     scalar2=0.0,
                     op0=ALU.mult,
                     op1=ALU.add,
@@ -213,7 +214,7 @@ def tile_dygcn_pa_t_kernel(tc, A, x, out):
             nc.vector.tensor_tensor(
                 out=live["t2_grouped", b][:].rearrange("p (c n t) -> p c n t", c=PACK, t=PACK)[:, c, :, :],
                 in0=live["squared", b, c][:].rearrange("p t n -> p n t"),
-                in1=eye_t2[:, c, :, :],
+                in1=half_eye[:, c, :, :],
                 op=ALU.subtract,
             )
 
@@ -237,8 +238,13 @@ def tile_dygcn_pa_t_kernel(tc, A, x, out):
 
         def store(b, which, h):
             result = results.tile([P, 2, FEATS], F32)
-            copy = nc.vector.tensor_copy if (b, which, h) == (GRAPHS - 1, 1, 1) else nc.scalar.copy
-            copy(out=result[:], in_=live["acc", b, h][:])
+            acc = live["acc", b, h][:]
+            if which == 0:
+                nc.scalar.copy(out=result[:], in_=acc)
+            elif (b, h) == (GRAPHS - 1, 1):
+                nc.vector.tensor_scalar(out=result[:], in0=acc, scalar1=2.0, scalar2=None, op0=ALU.mult)
+            else:
+                nc.scalar.activation(out=result[:], in_=acc, func=ACT.Copy, scale=2.0)
             nc.sync.dma_start(out=rows_by_node(out[b, which])[:, 2 * h : 2 * h + 2, :], in_=result[:])
 
         def quantise(b, name, width, begin=0, end=None):

@@ -18,6 +18,9 @@ P = 128
 PACK = 4
 
 SCALAR_RUNS = 56
+HALF = NODES // 2 + 36
+E_STEP = 3 * HALF
+U_STEP = 4 * HALF + P
 LOADS_AHEAD = 4
 
 FLOPS = GRAPHS * 2 * (NODES * NODES * NODES + 2 * NODES * NODES * FEATS)
@@ -29,6 +32,10 @@ def rows_by_node(dram):
 
 def in_column_order(row):
     return row.rearrange("p (u q e) -> p u q e", u=2, e=2)
+
+
+def halves(pos, t):
+    return pos[:, 2 * HALF * t : 2 * HALF * (t + 1)].rearrange("p (e w) -> p e w", e=2)[:, :, 0 : NODES // 2]
 
 
 def in_runs(view):
@@ -84,11 +91,11 @@ def tile_dygcn_pa_t_kernel(tc, A, x, out):
 
         def positive_part(b):
             a_raw = live["a_raw", b]
-            pos = work.tile([P, 4 * PACK, P], F32)
+            pos = work.tile([P, U_STEP + 2 * E_STEP], F32)
             rowsum = small.tile([P, PACK], F32)
             for t in range(PACK):
                 raw = a_raw[:, t, :].rearrange("p (q u e) -> p e u q", u=2, e=2)
-                pos_row = pos[:, 4 * t : 4 * t + 4, :].rearrange("p (e u) q -> p e u q", e=2)
+                pos_row = halves(pos, t).rearrange("p e (u q) -> p e u q", u=2)
                 if t in relu_on_vector(b):
                     nc.vector.tensor_scalar(
                         out=pos_row,
@@ -108,7 +115,8 @@ def tile_dygcn_pa_t_kernel(tc, A, x, out):
 
 
         def add_identity(b, u):
-            diag = live["pos", b][:, 9 * u : 9 * u + 7 : 6, :]
+            pair = live["pos", b][:, U_STEP * u : U_STEP * u + 2 * E_STEP].rearrange("p (e w) -> p e w", e=2)
+            diag = pair[:, :, 0:P]
             nc.gpsimd.tensor_tensor(out=diag, in0=diag, in1=ident_x2[:], op=ALU.add)
 
         def inverse_root(b):
@@ -133,7 +141,7 @@ def tile_dygcn_pa_t_kernel(tc, A, x, out):
             for t in slots:
                 nc.vector.scalar_tensor_tensor(
                     out=live["a_hat", b][:, t, :].rearrange("p (w e) -> p w e", e=2),
-                    in0=live["pos", b][:, 4 * t : 4 * t + 4, :].rearrange("p (e u) q -> p (u q) e", e=2),
+                    in0=halves(live["pos", b], t).rearrange("p e w -> p w e"),
                     scalar=live["r", b][:, t : t + 1],
                     in1=live["r_row", b][:].rearrange("p (w e) -> p w e", e=2),
                     op0=ALU.mult,
@@ -148,6 +156,8 @@ def tile_dygcn_pa_t_kernel(tc, A, x, out):
             to, source = in_runs(grouped), in_runs(columns)
             if b == 0:
                 nc.vector.tensor_copy(out=to, in_=source)
+            elif e == 0 and b == GRAPHS - 1:
+                nc.scalar.copy(out=to, in_=source)
             elif e == 0:
                 nc.scalar.copy(out=to[:, :SCALAR_RUNS], in_=source[:, :SCALAR_RUNS])
                 nc.vector.tensor_copy(out=to[:, SCALAR_RUNS:], in_=source[:, SCALAR_RUNS:])
@@ -300,6 +310,8 @@ def tile_dygcn_pa_t_kernel(tc, A, x, out):
                         quantise(back, "t2", NODES, 0, NODES // 2)
                     square(back, 3)
                     chebyshev(back, 3)
+                    if back == GRAPHS - 1:
+                        quantise(back, "t2", NODES, NODES // 2, 3 * NODES // 4)
                 if 0 <= middle < GRAPHS:
                     regroup_left(middle, 0)
                     regroup_left(middle, 1)
@@ -315,7 +327,7 @@ def tile_dygcn_pa_t_kernel(tc, A, x, out):
                 if 0 <= middle < GRAPHS:
                     quantise(middle, "left", NODES)
                 if 0 <= back < GRAPHS:
-                    quantise(back, "t2", NODES, NODES // 2 if back == GRAPHS - 1 else 0)
+                    quantise(back, "t2", NODES, 3 * NODES // 4 if back == GRAPHS - 1 else 0)
                 if 0 <= middle < GRAPHS:
                     quantise(middle, "right", NODES)
                     quantise(middle, "x", FEATS)

from contextlib import ExitStack

import concourse.mybir as mybir
from concourse.masks import make_identity

F32 = mybir.dt.float32
BF16 = mybir.dt.bfloat16
U32 = mybir.dt.uint32
U8 = mybir.dt.uint8
FP8X4 = mybir.dt.float8_e4m3fn_x4
ALU = mybir.AluOpType
ACT = mybir.ActivationFunctionType

GRAPHS = 16
NODES = 512
FEATS = 256
P = 128
PACK = 4

SCALAR_RUNS = 56
HALF = NODES // 2 + 36
E_STEP = 3 * HALF
U_STEP = 4 * HALF + P
LOADS_AHEAD = 4

FLOPS = GRAPHS * 2 * (NODES * NODES * NODES + 2 * NODES * NODES * FEATS)


def rows_by_node(dram):
    return dram.rearrange("(p t) w -> p t w", t=PACK)


def in_column_order(row):
    return row.rearrange("p (u q e) -> p u q e", u=2, e=2)


def halves(pos, t):
    return pos[:, 2 * HALF * t : 2 * HALF * (t + 1)].rearrange("p (e w) -> p e w", e=2)[:, :, 0 : NODES // 2]


def in_runs(view):
    return view.rearrange("p (c i) s -> p c s i", i=4)


def relu_on_vector(b):
    return {0: (1, 3)}.get(b, ())


def tile_dygcn_pa_t_kernel(tc, A, x, out):
    nc = tc.nc
    with ExitStack() as stack:
        const = stack.enter_context(tc.tile_pool(name="const", bufs=1))
        loads = stack.enter_context(tc.tile_pool(name="loads", bufs=LOADS_AHEAD + 2))
        work = stack.enter_context(tc.tile_pool(name="work", bufs=3))
        small = stack.enter_context(tc.tile_pool(name="small", bufs=4))
        mx = stack.enter_context(tc.tile_pool(name="mx", bufs=4))
        results = stack.enter_context(tc.tile_pool(name="results", bufs=8))
        x_work = stack.enter_context(tc.tile_pool(name="x_work", bufs=1))
        ps_row = stack.enter_context(tc.psum_pool(name="ps_row", bufs=1))
        ps_tr = stack.enter_context(tc.psum_pool(name="ps_tr", bufs=2))
        ps_t2 = stack.enter_context(tc.psum_pool(name="ps_t2", bufs=3))
        ps_out = stack.enter_context(tc.psum_pool(name="ps_out", bufs=2))

        one = const.tile([P, 1], F32)
        nc.vector.memset(one[:], 1.0)
        root_one = const.tile([P, 1], F32)
        nc.scalar.activation(out=root_one[:], in_=one[:], func=ACT.Abs_reciprocal_sqrt)

        ident_f32 = const.tile([P, P], F32)
        make_identity(nc, ident_f32[:])
        ident_x2 = const.tile([P, 2, P], F32)
        for e in range(2):
            nc.vector.tensor_copy(out=ident_x2[:, e, :], in_=ident_f32[:])
        half_eye = const.tile([P, PACK, P, PACK], BF16)
        nc.vector.memset(half_eye[:], 0.0)
        for c in range(PACK):
            nc.gpsimd.tensor_scalar(
                out=half_eye[:, c, :, c], in0=ident_f32[:], scalar1=0.5, scalar2=0.0, op0=ALU.mult, op1=ALU.add
            )

        live = {}

        def load(b):
            a_raw = loads.tile([P, PACK, NODES], BF16)
            for h in range(2):
                nc.sync.dma_start(out=a_raw[:, 2 * h : 2 * h + 2, :], in_=rows_by_node(A[b])[:, 2 * h : 2 * h + 2, :])
            x_raw = loads.tile([P, PACK, FEATS], BF16)
            nc.sync.dma_start(out=x_raw[:], in_=rows_by_node(x[b]))
            live["a_raw", b] = a_raw
            live["x_raw", b] = x_raw

        def positive_part(b):
            a_raw = live["a_raw", b]
            pos = work.tile([P, U_STEP + 2 * E_STEP], F32)
            rowsum = small.tile([P, PACK], F32)
            for t in range(PACK):
                raw = a_raw[:, t, :].rearrange("p (q u e) -> p e u q", u=2, e=2)
                pos_row = halves(pos, t).rearrange("p e (u q) -> p e u q", u=2)
                if t in relu_on_vector(b):
                    nc.vector.tensor_scalar(
                        out=pos_row,
                        in0=raw,
                        scalar1=0.0,
                        scalar2=None,
                        op0=ALU.max,
                        op1=ALU.add,
                        accum_out=rowsum[:, t : t + 1],
                    )
                else:
                    nc.scalar.activation(
                        out=pos_row, in_=raw, func=ACT.Relu, accum_out=rowsum[:, t : t + 1]
                    )
            live["pos", b] = pos
            live["rowsum", b] = rowsum


        def add_identity(b, u):
            pair = live["pos", b][:, U_STEP * u : U_STEP * u + 2 * E_STEP].rearrange("p (e w) -> p e w", e=2)
            diag = pair[:, :, 0:P]
            nc.gpsimd.tensor_tensor(out=diag, in0=diag, in1=ident_x2[:], op=ALU.add)

        def inverse_root(b):
            r = small.tile([P, PACK], F32)
            nc.scalar.activation(out=r[:], in_=live["rowsum", b][:], func=ACT.Abs_reciprocal_sqrt, bias=1.0)
            live["r", b] = r

        def spread_r(b):
            r = live["r", b]
            r_row = ps_row.tile([P, NODES], F32)
            for t in range(PACK):
                nc.tensor.transpose(
                    in_column_order(r_row[:])[:, t // 2, :, t % 2],
                    r[:, t : t + 1].to_broadcast([P, P]),
                    ident_f32[:],
                )
            live["r_row", b] = r_row

        def scale(b, slots=range(PACK)):
            if 0 in slots:
                live["a_hat", b] = work.tile([P, PACK, NODES], BF16, name="a_hat")
            for t in slots:
                nc.vector.scalar_tensor_tensor(
                    out=live["a_hat", b][:, t, :].rearrange("p (w e) -> p w e", e=2),
                    in0=halves(live["pos", b], t).rearrange("p e w -> p w e"),
                    scalar=live["r", b][:, t : t + 1],
                    in1=live["r_row", b][:].rearrange("p (w e) -> p w e", e=2),
                    op0=ALU.mult,
                    op1=ALU.mult,
                )

        def regroup_right(b, e):
            if ("right_grouped", b) not in live:
                live["right_grouped", b] = work.tile([P, NODES * PACK], BF16, align_bytes=64, name="right_grouped")
            grouped = live["right_grouped", b][:].rearrange("p (e w s) -> p e w s", e=2, s=PACK)[:, e, :, :]
            columns = live["a_hat", b][:].rearrange("p s (w e) -> p e w s", e=2)[:, e, :, :]
            to, source = in_runs(grouped), in_runs(columns)
            if b == 0:
                nc.vector.tensor_copy(out=to, in_=source)
            elif e == 0 and b == GRAPHS - 1:
                nc.scalar.copy(out=to, in_=source)
            elif e == 0:
                nc.scalar.copy(out=to[:, :SCALAR_RUNS], in_=source[:, :SCALAR_RUNS])
                nc.vector.tensor_copy(out=to[:, SCALAR_RUNS:], in_=source[:, SCALAR_RUNS:])
            else:
                nc.gpsimd.tensor_scalar(
                    out=to,
                    in0=source,
                    scalar1=1.0,
                    scalar2=0.0,
                    op0=ALU.mult,
                    op1=ALU.add,
                )

        def flip(b, h):
            flipped = ps_tr.tile([P, 2, 2, P], F32)
            for c in range(2):
                row_words = live["a_hat", b][:, 2 * h + c, :].bitcast(F32)
                for u in range(2):
                    nc.tensor.transpose(flipped[:, c, u, :], row_words[:, u * P : (u + 1) * P], ident_f32[:])
            live["flipped", b, h] = flipped

        def regroup_left(b, h):
            if h == 0:
                live["left_grouped", b] = work.tile([P, NODES * PACK], BF16, align_bytes=64, name="left_grouped")
            left_words = live["left_grouped", b][:].bitcast(F32).rearrange("p (h c n u) -> p h c n u", h=2, c=2, u=2)
            nc.scalar.copy(
                out=left_words[:, h, :, :, :], in_=live["flipped", b, h][:].rearrange("p c u n -> p c n u")
            )

        def regroup_x(b):
            x_grouped = x_work.tile([P, FEATS * PACK], BF16, align_bytes=64)
            nc.gpsimd.tensor_scalar(
                out=in_runs(x_grouped[:].rearrange("p (f s) -> p f s", s=PACK)),
                in0=in_runs(live["x_raw", b][:].rearrange("p s f -> p f s")),
                scalar1=1.0,
                scalar2=0.0,
                op0=ALU.mult,
                op1=ALU.add,
            )
            live["x_grouped", b] = x_grouped

        def square(b, c):
            right_codes, right_scales = live["right", b]
            left_codes, left_scales = live["left", b]
            n_cols = slice(c * P, (c + 1) * P)
            squared = ps_t2.tile([P, PACK, P], F32)
            for t in range(PACK):
                block = 2 * (t % 2) + t // 2
                j_cols = slice(block * P, (block + 1) * P)
                nc.tensor.matmul_mx(
                    out=squared[:, t, :],
                    lhsT=right_codes[:, j_cols].bitcast(FP8X4),
                    lhsT_scale=right_scales[:, j_cols],
                    rhs=left_codes[:, n_cols].bitcast(FP8X4),
                    rhs_scale=left_scales[:, n_cols],
                    start=True,
                    stop=True,
                )
            live["squared", b, c] = squared

        def chebyshev(b, c):
            if c == 0:
                live["t2_grouped", b] = work.tile([P, NODES * PACK], BF16, align_bytes=64, name="t2_grouped")
            nc.vector.tensor_tensor(
                out=live["t2_grouped", b][:].rearrange("p (c n t) -> p c n t", c=PACK, t=PACK)[:, c, :, :],
                in0=live["squared", b, c][:].rearrange("p t n -> p n t"),
                in1=half_eye[:, c, :, :],
                op=ALU.subtract,
            )

        def times_x(b, name):
            codes, scales = live[name, b]
            x_codes, x_scales = live["x", b]
            for h in range(2):
                acc = ps_out.tile([P, 2, FEATS], F32)
                for c in range(2):
                    n_cols = slice((2 * h + c) * P, (2 * h + c + 1) * P)
                    nc.tensor.matmul_mx(
                        out=acc[:, c, :],
                        lhsT=codes[:, n_cols].bitcast(FP8X4),
                        lhsT_scale=scales[:, n_cols],
                        rhs=x_codes[:].bitcast(FP8X4),
                        rhs_scale=x_scales[:],
                        start=True,
                        stop=True,
                    )
                live["acc", b, h] = acc

        def store(b, which, h):
            result = results.tile([P, 2, FEATS], F32)
            acc = live["acc", b, h][:]
            if which == 0:
                nc.scalar.copy(out=result[:], in_=acc)
            elif (b, h) == (GRAPHS - 1, 1):
                nc.vector.tensor_scalar(out=result[:], in0=acc, scalar1=2.0, scalar2=None, op0=ALU.mult)
            else:
                nc.scalar.activation(out=result[:], in_=acc, func=ACT.Copy, scale=2.0)
            nc.sync.dma_start(out=rows_by_node(out[b, which])[:, 2 * h : 2 * h + 2, :], in_=result[:])

        def quantise(b, name, width, begin=0, end=None):
            end = width if end is None else end
            if begin == 0:
                codes = mx.tile([P, width], U32, align_bytes=64, name=name + "_codes")
                scales = mx.tile([P, width], U8, align_bytes=64, name=name + "_scales")
                live[name, b] = codes, scales
            codes, scales = live[name, b]
            nc.vector.quantize_mx(
                out=codes[:, begin:end].bitcast(FP8X4),
                scales=scales[:, begin:end],
                in_=live[name + "_grouped", b][:, begin * PACK : end * PACK],
            )

        with tc.manual_schedule():
            for b in range(LOADS_AHEAD):
                load(b)
            for i in range(-2, GRAPHS + 1):
                front, middle, back, last = i + 2, i + 1, i, i - 1
                if front + LOADS_AHEAD < GRAPHS:
                    load(front + LOADS_AHEAD)
                if 0 <= last:
                    times_x(last, "t2")
                if 0 <= middle < GRAPHS:
                    regroup_x(middle)
                    scale(middle)
                if front < GRAPHS:
                    positive_part(front)
                    add_identity(front, 0)
                if 0 <= middle < GRAPHS:
                    regroup_right(middle, 1)
                if front < GRAPHS:
                    add_identity(front, 1)
                if 0 <= back < GRAPHS:
                    square(back, 0)
                    square(back, 1)
                    square(back, 2)
                if 0 <= last:
                    store(last, 1, 0)
                if front < GRAPHS:
                    inverse_root(front)
                if 0 <= last:
                    store(last, 1, 1)
                if 0 <= middle < GRAPHS:
                    flip(middle, 0)
                    flip(middle, 1)
                if 0 <= back < GRAPHS:
                    chebyshev(back, 0)
                    chebyshev(back, 1)
                    chebyshev(back, 2)
                    if back == GRAPHS - 1:
                        quantise(back, "t2", NODES, 0, NODES // 2)
                    square(back, 3)
                    chebyshev(back, 3)
                    if back == GRAPHS - 1:
                        quantise(back, "t2", NODES, NODES // 2, 3 * NODES // 4)
                if 0 <= middle < GRAPHS:
                    regroup_left(middle, 0)
                    regroup_left(middle, 1)
                if 0 <= back < GRAPHS:
                    times_x(back, "left")
                if front < GRAPHS:
                    spread_r(front)
                if 0 <= middle < GRAPHS:
                    regroup_right(middle, 0)
                if 0 <= back < GRAPHS:
                    store(back, 0, 0)
                    store(back, 0, 1)
                if 0 <= middle < GRAPHS:
                    quantise(middle, "left", NODES)
                if 0 <= back < GRAPHS:
                    quantise(back, "t2", NODES, 3 * NODES // 4 if back == GRAPHS - 1 else 0)
                if 0 <= middle < GRAPHS:
                    quantise(middle, "right", NODES)
                    quantise(middle, "x", FEATS)
